import numpy as np
import ml_dtypes


def mxq(x, axis, fmt="e4m3"):
    dtype, down = {"e4m3": (ml_dtypes.float8_e4m3fn, 7), "e5m2": (ml_dtypes.float8_e5m2, 14)}[fmt]
    v = np.moveaxis(np.asarray(x, np.float32).astype(ml_dtypes.bfloat16).astype(np.float64), axis, -1)
    blocks = v.reshape(v.shape[:-1] + (-1, 32))
    amax = np.abs(blocks).max(-1, keepdims=True)
    byte = np.maximum(np.where(amax > 0, np.frexp(amax)[1] - 1 + 127, 0) - down, 1)
    scale = np.exp2(byte - 127.0)
    codes = (blocks / scale).astype(np.float32).astype(dtype).astype(np.float64)
    return np.moveaxis((codes * scale).reshape(v.shape), -1, axis)


WIDE = False


def mx_kscale(k):
    if not WIDE:
        return np.ones(k)
    levels = np.array([10, -10, 5, -5, 0])
    if k % 512:
        return np.exp2(np.random.permutation(np.resize(levels, k // 32))).repeat(32)
    a = np.empty((k // 512, 16))
    for p in range(k // 512):
        a[p, :8] = np.random.permutation(np.resize(levels, 8))
        for g in range(8):
            far = levels[np.abs(levels - a[p, g]) >= 10]
            a[p, g + 8] = far[np.random.randint(len(far))]
    return np.exp2(a.ravel()).repeat(32)


BF16 = ml_dtypes.bfloat16


def bf(x):
    return np.asarray(x, np.float32).astype(BF16)


def f64(x):
    return np.asarray(x).astype(np.float64)


B, S, DV, D, H, A = 2, 256, 1024, 1024, 8, 64
LN_EPS = 1e-3


def setup_inputs():
    s = mx_kscale(DV)
    return {
        "attn": bf(np.random.standard_normal((B, H, S, DV)) * 0.4 * s),
        "Wo": bf(np.random.standard_normal((H, DV, D)) * 0.6 / np.sqrt(DV * H) / s[None, :, None]),
        "bo": bf(np.random.standard_normal((H, D)) * 0.12 / np.sqrt(H)),
        "query_inputs": bf(np.random.standard_normal((B, S, D)) * 0.1),
        "gamma": bf(1.0 + 0.1 * np.random.standard_normal(D)),
        "beta": bf(0.1 * np.random.standard_normal(D)),
    }


def core(attn, Wo, bo, query_inputs, gamma, beta):
    pre = mxq(f64(attn), 3, "e4m3") @ mxq(f64(Wo), 1, "e4m3")
    head_out = np.maximum(pre + f64(bo)[None, :, None, :], 0.0)
    x = f64(query_inputs) + head_out.sum(axis=1)
    mean = x.mean(axis=-1, keepdims=True)
    var = x.var(axis=-1, keepdims=True)
    return f64(gamma) * (x - mean) / np.sqrt(var + LN_EPS) + f64(beta)


def e4m3fn_bytes(y):
    return np.clip(np.asarray(y, np.float64), -448.0, 448.0).astype(np.float32).astype(ml_dtypes.float8_e4m3fn).view(np.uint8)


Y_SCALE = 220.0


def reference(attn, Wo, bo, query_inputs, gamma, beta):
    out = core(attn, Wo, bo, query_inputs, gamma, beta)
    return out, e4m3fn_bytes(out * Y_SCALE)

@@ -1,0 +1,362 @@
+from contextlib import ExitStack
+
+import concourse.masks as masks
+import concourse.mybir as mybir
+
+B, H, S, DV, D = 2, 8, 256, 1024, 1024
+FLOPS = 2 * B * H * S * DV * D
+
+F32 = mybir.dt.float32
+BF16 = mybir.dt.bfloat16
+U32 = mybir.dt.uint32
+U8 = mybir.dt.uint8
+FP8X4 = mybir.dt.float8_e4m3fn_x4
+FP8 = mybir.dt.float8_e4m3fn
+ALU = mybir.AluOpType
+ACT = mybir.ActivationFunctionType
+
+P = 128
+TOK = B * S
+NT = TOK // P
+ND = D // P
+NG = DV // 512
+LN_EPS = 1e-3
+Y_SCALE = 220.0
+AHEAD = 3
+
+
+def shares(h, g):
+    if h == 0:
+        return "VVVVVSSS"
+    if h == 1:
+        return "VVVSSSSS" if g == 0 else "VVSSSSGG"
+    if h >= 6:
+        return "VSSSGGGG" if g == 0 else "VVSSSSGG"
+    return "SSSSGGGG" if g == 0 else "VSSSSSGG"
+
+
+def runs(h, g):
+    s = shares(h, g)
+    out = []
+    i = 0
+    while i < 8:
+        k = i
+        while k < 8 and s[k] == s[i]:
+            k += 1
+        out.append((s[i], i, k - i))
+        i = k
+    return out
+
+
+def chunks(n):
+    out = []
+    for w in (8, 4, 2, 1):
+        while n >= w:
+            out.append(w)
+            n -= w
+    return out
+
+
+def on_scalar(h, j):
+    return (h == 6 and j < 4) or (h == 7 and j >= 4)
+
+
+def tile_multiheadattentionunit_pa_kernel(tc, attn, Wo, bo, query_inputs, gamma, beta, out_0, out_1):
+    nc = tc.nc
+    with ExitStack() as ctx:
+        const = ctx.enter_context(tc.tile_pool(name="const", bufs=1))
+        wpool = ctx.enter_context(tc.tile_pool(name="wpool", bufs=2 * AHEAD))
+        apool = ctx.enter_context(tc.tile_pool(name="apool", bufs=AHEAD))
+        upool = ctx.enter_context(tc.tile_pool(name="upool", bufs=4))
+        cpool = ctx.enter_context(tc.tile_pool(name="cpool", bufs=4))
+        small = ctx.enter_context(tc.tile_pool(name="small", bufs=4))
+        tailp = ctx.enter_context(tc.tile_pool(name="tailp", bufs=2))
+        psum = ctx.enter_context(tc.psum_pool(name="psum", bufs=4))
+        ctx.enter_context(tc.manual_schedule(engines={mybir.EngineType.DVE, mybir.EngineType.Pool}))
+
+        a_raw = {}
+        w_raw = {}
+        tps = {}
+        a_grp = {}
+        a_code = {}
+        a_scale = {}
+        units = {}
+        w_code = {}
+        w_scale = {}
+        mxs = {}
+        xts = {}
+
+        def ok(h):
+            return 0 <= h < H
+
+        def load_a(h):
+            t = apool.tile([P, NT, DV], BF16, name="a_raw", tag="a_raw")
+            a_raw[h] = t
+            for b in range(B):
+                nc.sync.dma_start(out=t[:, 2 * b : 2 * b + 2, :], in_=attn[b, h].rearrange("(i p) k -> p i k", p=P))
+
+        def load_w(h):
+            for g in range(NG):
+                t = wpool.tile([P, 4, D], BF16, name="w_raw", tag="w_raw")
+                w_raw[(h, g)] = t
+                nc.sync.dma_start(out=t[:], in_=Wo[h, 512 * g : 512 * (g + 1), :].rearrange("(p j) d -> p j d", j=4))
+
+        load_a(0)
+        cst = const.tile([P, P], BF16, name="cst")
+        nc.vector.memset(cst[:], 0.0)
+        nc.sync.dma_start(out=cst[0:64, :], in_=bo.rearrange("h (j p) -> (h j) p", p=P))
+        load_w(0)
+        for h in range(1, AHEAD):
+            load_a(h)
+            load_w(h)
+
+        ident_f = const.tile([P, P], F32, name="ident_f")
+        masks.make_identity(nc, ident_f[:])
+        ident_b = const.tile([P, P], BF16, name="ident_b")
+        masks.make_identity(nc, ident_b[:])
+        warm = const.tile([P, 1], F32, name="warm")
+        nc.vector.memset(warm[:], 1.0)
+        warm2 = const.tile([P, 1], F32, name="warm2")
+        nc.scalar.activation(out=warm2[:], in_=warm[:], func=ACT.Sqrt)
+        eps_t = const.tile([P, 1], F32, name="eps_t")
+        nc.vector.tensor_scalar(out=eps_t[:], in0=warm[:], scalar1=LN_EPS, scalar2=None, op0=ALU.mult)
+
+        acc = const.tile([P, ND, TOK], F32, name="acc")
+        acc2 = const.tile([P, ND, TOK], F32, name="acc2")
+        negb = const.tile([P, H * ND], F32, name="negb")
+        posb = const.tile([P, H * ND], F32, name="posb")
+        bsum = const.tile([P, ND], F32, name="bsum")
+        bsv = const.tile([P, ND], F32, name="bsv")
+        gamma_b = const.tile([P, D], BF16, name="gamma_b")
+        beta_b = const.tile([P, D], BF16, name="beta_b")
+        q_raw = const.tile([P, NT, D], BF16, name="q_raw")
+
+        def transpose_a(h):
+            if not ok(h):
+                return
+            words = a_raw[h][:].bitcast(F32)
+            for b in range(B):
+                for g in range(NG):
+                    tp = psum.tile([P, 2, 256], F32, name="tp", tag="tp")
+                    tps[(h, g, b)] = tp
+                    for ii in range(2):
+                        for u in range(2):
+                            nc.tensor.transpose(
+                                tp[:, u, P * ii : P * (ii + 1)],
+                                words[:, 2 * b + ii, 256 * g + u : 256 * (g + 1) : 2],
+                                ident_f[:],
+                            )
+
+        def interleave(h, g, e):
+            if not ok(h):
+                return
+            for eng, p0, n in runs(h, g):
+                if eng != e:
+                    continue
+                t = upool.tile([P, P * n, 4], BF16, name="unit" + e, tag="unit" + e,
+                               bufs={"S": 4, "V": 2, "G": 1}[e], align_bytes=64)
+                units[(h, g, p0)] = t
+                src = w_raw[(h, g)][:, :, P * p0 : P * (p0 + n)].rearrange("p j d -> p d j")
+                if e == "S":
+                    nc.scalar.copy(out=t[:], in_=src)
+                elif e == "V":
+                    nc.vector.tensor_copy(out=t[:], in_=src)
+                else:
+                    nc.gpsimd.tensor_scalar(out=t[:], in0=src, scalar1=1.0, scalar2=0.0, op0=ALU.mult, op1=ALU.add)
+
+        def prepare_scalar(h):
+            if not ok(h):
+                return
+            w32 = {}
+            for g in range(NG):
+                t = cpool.tile([P, 4 * TOK], BF16, name="a_grp", tag="a_grp", align_bytes=64)
+                a_grp[(h, g)] = t
+                w32[g] = t[:].bitcast(F32).rearrange("p (r u) -> p r u", u=2)
+            for b in range(B):
+                for g in range(NG):
+                    nc.scalar.copy(
+                        out=w32[g][:, 256 * b : 256 * (b + 1), :],
+                        in_=tps[(h, g, b)][:].rearrange("p u r -> p r u"),
+                    )
+            for g in range(NG):
+                interleave(h, g, "S")
+
+        def quantize(h, g):
+            if not ok(h):
+                return
+            interleave(h, g, "V")
+            c = cpool.tile([P, TOK], U32, name="a_code", tag="a_code", align_bytes=64)
+            s = cpool.tile([P, TOK], U8, name="a_scale", tag="a_scale", align_bytes=64)
+            a_code[(h, g)] = c
+            a_scale[(h, g)] = s
+            nc.vector.quantize_mx(out=c[:].bitcast(FP8X4), scales=s[:], in_=a_grp[(h, g)][:])
+            wc = cpool.tile([P, D], U32, name="w_code", tag="w_code", align_bytes=64)
+            ws = cpool.tile([P, D], U8, name="w_scale", tag="w_scale", align_bytes=64)
+            w_code[(h, g)] = wc
+            w_scale[(h, g)] = ws
+            for e in ("S", "V", "G"):
+                for eng, p0, n in runs(h, g):
+                    if eng != e:
+                        continue
+                    o = 0
+                    for w in chunks(n):
+                        cols = slice(P * (p0 + o), P * (p0 + o + w))
+                        nc.vector.quantize_mx(
+                            out=wc[:, cols].bitcast(FP8X4),
+                            scales=ws[:, cols],
+                            in_=units[(h, g, p0)][:, P * o : P * (o + w), :].rearrange("p d j -> p (d j)"),
+                        )
+                        o += w
+
+        def matmuls(h, j0, j1):
+            if not ok(h):
+                return
+            for j in range(j0, j1):
+                ps = psum.tile([P, TOK], F32, name="mx", tag="mx")
+                mxs[(h, j)] = ps
+                cols = slice(P * j, P * (j + 1))
+                for g in range(NG):
+                    nc.tensor.matmul_mx(
+                        out=ps[:],
+                        lhsT=w_code[(h, g)][:, cols].bitcast(FP8X4),
+                        lhsT_scale=w_scale[(h, g)][:, cols],
+                        rhs=a_code[(h, g)][:].bitcast(FP8X4),
+                        rhs_scale=a_scale[(h, g)][:],
+                        start=(g == 0),
+                        stop=(g == NG - 1),
+                    )
+
+        def epilogue(h, j0, j1):
+            if not ok(h):
+                return
+            for j in range(j0, j1):
+                col = slice(ND * h + j, ND * h + j + 1)
+                if on_scalar(h, j):
+                    nc.scalar.activation(out=acc2[:, j, :], in_=mxs[(h, j)][:], func=ACT.Relu, bias=posb[:, col], scale=1.0)
+                elif h == 0:
+                    nc.vector.tensor_scalar(out=acc[:, j, :], in0=mxs[(h, j)][:], scalar1=negb[:, col],
+                                            scalar2=bsv[:, j : j + 1], op0=ALU.max, op1=ALU.add)
+                else:
+                    nc.vector.scalar_tensor_tensor(out=acc[:, j, :], in0=mxs[(h, j)][:], scalar=negb[:, col],
+                                                   in1=acc[:, j, :], op0=ALU.max, op1=ALU.add)
+
+        def xt_open(i, hf, tag):
+            xt = psum.tile([P, 512], F32, name="xt", tag=tag)
+            xts[(i, hf)] = xt
+            nc.tensor.matmul(out=xt[:], lhsT=ident_b[:], rhs=q_raw[:, i, 512 * hf : 512 * (hf + 1)], start=True, stop=False)
+
+        def xt_add(i, hf, chain, last):
+            xt = xts[(i, hf)]
+            for jj in range(4):
+                nc.tensor.matmul(
+                    out=xt[:, P * jj : P * (jj + 1)],
+                    lhsT=chain[:, 4 * hf + jj, P * i : P * (i + 1)],
+                    rhs=ident_f[:],
+                    is_transpose=True,
+                    start=False,
+                    stop=(last and jj == 3),
+                )
+
+        cps = psum.tile([P, P], BF16, name="cps", tag="tp")
+        nc.tensor.transpose(cps[:], cst[:], ident_b[:])
+        nc.vector.tensor_scalar(out=negb[:], in0=cps[:, 0 : H * ND], scalar1=-1.0, scalar2=None, op0=ALU.mult)
+        nc.vector.tensor_copy(out=posb[:], in_=cps[:, 0 : H * ND])
+        nc.vector.tensor_reduce(out=bsum[:], in_=cps[:, 0 : H * ND].rearrange("p (h j) -> p j h", h=H),
+                                axis=mybir.AxisListType.X, op=ALU.add)
+        nc.vector.tensor_tensor(out=bsv[:, 0:4], in0=bsum[:, 0:4], in1=posb[:, 6 * ND : 6 * ND + 4], op=ALU.subtract)
+        nc.vector.tensor_tensor(out=bsv[:, 4:8], in0=bsum[:, 4:8], in1=posb[:, 7 * ND + 4 : 7 * ND + 8], op=ALU.subtract)
+
+        transpose_a(0)
+        prepare_scalar(0)
+        transpose_a(1)
+        interleave(0, 0, "G")
+        quantize(0, 0)
+        interleave(0, 1, "G")
+        for h in range(H):
+            hl = h + AHEAD
+            if ok(hl):
+                load_a(hl)
+                load_w(hl)
+            if hl == H:
+                nc.sync.dma_start(out=gamma_b[:], in_=gamma.partition_broadcast(P))
+                nc.sync.dma_start(out=beta_b[:], in_=beta.partition_broadcast(P))
+                for b in range(B):
+                    nc.sync.dma_start(out=q_raw[:, 2 * b : 2 * b + 2, :], in_=query_inputs[b].rearrange("(i p) d -> p i d", p=P))
+            prepare_scalar(h + 1)
+            quantize(h, 1)
+            interleave(h + 1, 0, "G")
+            epilogue(h - 1, 6, 8)
+            matmuls(h, 0, 4)
+            transpose_a(h + 2)
+            if h == H - 1:
+                for i in range(2):
+                    xt_open(i, 0, "tp")
+                    xt_add(i, 0, acc2, False)
+                    xt_open(i, 1, "tp")
+                    xt_add(i, 1, acc, False)
+            epilogue(h, 0, 3)
+            matmuls(h, 4, 7)
+            quantize(h + 1, 0)
+            interleave(h + 1, 1, "G")
+            epilogue(h, 3, 6)
+            matmuls(h, 7, 8)
+        epilogue(H - 1, 6, 8)
+
+        for i in range(NT):
+            if i >= 2:
+                xt_open(i, 0, "mx")
+                xt_add(i, 0, acc2, False)
+                xt_open(i, 1, "mx")
+                xt_add(i, 1, acc, False)
+            xt_add(i, 0, acc, True)
+            xt_add(i, 1, acc2, True)
+
+        shift = {}
+        spread = {}
+        for i in range(NT):
+            if i < 2:
+                st = small.tile([P, 2, 6], F32, name="st", tag="st")
+                for hf in range(2):
+                    nc.vector.bn_stats(out=st[:, hf, :], in_=xts[(i, hf)][:])
+                mv = small.tile([P, 2], F32, name="mv", tag="mv")
+                nc.vector.bn_aggr(out=mv[:], in_=st[:].rearrange("p a b -> p (a b)"))
+                shift[i] = (mv[:, 0:1], ALU.subtract)
+                spread[i] = mv[:, 1:2]
+            else:
+                sm = small.tile([P, 2], F32, name="sm", tag="sm")
+                for hf in range(2):
+                    junk = tailp.tile([P, 512], F32, name="junk", tag="junk")
+                    nc.scalar.activation(out=junk[:], in_=xts[(i, hf)][:], func=ACT.Copy, accum_out=sm[:, hf : hf + 1])
+                nm = small.tile([P, 1], F32, name="nm", tag="nm")
+                nc.gpsimd.tensor_scalar(out=nm[:], in0=sm[:, 0:1], scalar1=sm[:, 1:2], scalar2=-1.0 / D, op0=ALU.add, op1=ALU.mult)
+                sq = small.tile([P, 2], F32, name="sq", tag="sq")
+                for hf in range(2):
+                    junk = tailp.tile([P, 512], F32, name="junk", tag="junk")
+                    nc.scalar.activation(out=junk[:], in_=xts[(i, hf)][:], func=ACT.Square, bias=nm[:, 0:1], scale=1.0,
+                                         accum_out=sq[:, hf : hf + 1])
+                vr = small.tile([P, 1], F32, name="vr", tag="vr")
+                nc.gpsimd.tensor_scalar(out=vr[:], in0=sq[:, 0:1], scalar1=sq[:, 1:2], scalar2=1.0 / D, op0=ALU.add, op1=ALU.mult)
+                shift[i] = (nm[:, 0:1], ALU.add)
+                spread[i] = vr[:, 0:1]
+        for i in range(NT):
+            sd = small.tile([P, 1], F32, name="sd", tag="sd")
+            nc.scalar.activation(out=sd[:], in_=spread[i], func=ACT.Sqrt, bias=eps_t[:, 0:1], scale=1.0)
+            rs = small.tile([P, 1], F32, name="rs", tag="rs")
+            nc.vector.reciprocal(out=rs[:], in_=sd[:])
+            t = tailp.tile([P, D], F32, name="t", tag="t")
+            for hf in range(2):
+                cols = slice(512 * hf, 512 * (hf + 1))
+                nc.vector.scalar_tensor_tensor(
+                    out=t[:, cols], in0=xts[(i, hf)][:], scalar=shift[i][0], in1=gamma_b[:, cols],
+                    op0=shift[i][1], op1=ALU.mult,
+                )
+            y = tailp.tile([P, D], F32, name="y", tag="y", bufs=3)
+            nc.vector.scalar_tensor_tensor(
+                out=y[:], in0=t[:], scalar=rs[:, 0:1], in1=beta_b[:], op0=ALU.mult, op1=ALU.add,
+            )
+            f8 = tailp.tile([P, D], FP8, name="f8", tag="f8", bufs=4)
+            nc.scalar.activation(out=f8[:], in_=y[:], func=ACT.Copy, scale=Y_SCALE, saturate=False)
+            b, i2 = divmod(i, 2)
+            rows = slice(P * i2, P * (i2 + 1))
+            nc.sync.dma_start(out=out_0[b, rows, :], in_=y[:])
+            nc.sync.dma_start(out=out_1[b, rows, :], in_=f8[:].bitcast(U8))

@@ -156,13 +156,14 @@ def tile_multiheadattentionunit_pa_kernel(tc, attn, Wo, bo, query_inputs, gamma,
                 t = upool.tile([P, P * n, 4], BF16, name="unit" + e, tag="unit" + e,
                                bufs={"S": 4, "V": 2, "G": 1}[e], align_bytes=64)
                 units[(h, g, p0)] = t
-                src = w_raw[(h, g)][:, :, P * p0 : P * (p0 + n)].rearrange("p j d -> p d j")
+                src = w_raw[(h, g)][:, :, P * p0 : P * (p0 + n)].rearrange("p j (c i) -> p c j i", i=4)
+                dst = t[:].rearrange("p (c i) j -> p c j i", i=4)
                 if e == "S":
-                    nc.scalar.copy(out=t[:], in_=src)
+                    nc.scalar.copy(out=dst, in_=src)
                 elif e == "V":
-                    nc.vector.tensor_copy(out=t[:], in_=src)
+                    nc.vector.tensor_copy(out=dst, in_=src)
                 else:
-                    nc.gpsimd.tensor_scalar(out=t[:], in0=src, scalar1=1.0, scalar2=0.0, op0=ALU.mult, op1=ALU.add)
+                    nc.gpsimd.tensor_scalar(out=dst, in0=src, scalar1=1.0, scalar2=0.0, op0=ALU.mult, op1=ALU.add)
 
         def prepare_scalar(h):
             if not ok(h):

@@ -29,10 +29,10 @@ def shares(h, g):
     if h == 0:
         return "VVVVVSSS"
     if h == 1:
-        return "VVVSSSSS" if g == 0 else "VVSSSSGG"
-    if h >= 6:
-        return "VSSSGGGG" if g == 0 else "VVSSSSGG"
-    return "SSSSGGGG" if g == 0 else "VSSSSSGG"
+        return "VVVSSSSS" if g == 0 else "SSSSSSGG"
+    if h == 2:
+        return "VVSSGGGG" if g == 0 else "SSSSSSGG"
+    return "SSSSGGGG" if g == 0 else "SSSSSSGG"
 
 
 def runs(h, g):
@@ -163,7 +163,8 @@ def tile_multiheadattentionunit_pa_kernel(tc, attn, Wo, bo, query_inputs, gamma,
                 elif e == "V":
                     nc.vector.tensor_copy(out=dst, in_=src)
                 else:
-                    nc.gpsimd.tensor_scalar(out=dst, in0=src, scalar1=1.0, scalar2=0.0, op0=ALU.mult, op1=ALU.add)
+                    nc.gpsimd.tensor_scalar(out=t[:], in0=w_raw[(h, g)][:, :, P * p0 : P * (p0 + n)].rearrange("p j d -> p d j"),
+                                            scalar1=1.0, scalar2=0.0, op0=ALU.mult, op1=ALU.add)
 
         def prepare_scalar(h):
             if not ok(h):
@@ -314,50 +315,69 @@ def tile_multiheadattentionunit_pa_kernel(tc, attn, Wo, bo, query_inputs, gamma,
 
         shift = {}
         spread = {}
-        for i in range(NT):
-            if i < 2:
-                st = small.tile([P, 2, 6], F32, name="st", tag="st")
-                for hf in range(2):
-                    nc.vector.bn_stats(out=st[:, hf, :], in_=xts[(i, hf)][:])
-                mv = small.tile([P, 2], F32, name="mv", tag="mv")
-                nc.vector.bn_aggr(out=mv[:], in_=st[:].rearrange("p a b -> p (a b)"))
-                shift[i] = (mv[:, 0:1], ALU.subtract)
-                spread[i] = mv[:, 1:2]
-            else:
-                sm = small.tile([P, 2], F32, name="sm", tag="sm")
-                for hf in range(2):
-                    junk = tailp.tile([P, 512], F32, name="junk", tag="junk")
-                    nc.scalar.activation(out=junk[:], in_=xts[(i, hf)][:], func=ACT.Copy, accum_out=sm[:, hf : hf + 1])
-                nm = small.tile([P, 1], F32, name="nm", tag="nm")
-                nc.gpsimd.tensor_scalar(out=nm[:], in0=sm[:, 0:1], scalar1=sm[:, 1:2], scalar2=-1.0 / D, op0=ALU.add, op1=ALU.mult)
-                sq = small.tile([P, 2], F32, name="sq", tag="sq")
-                for hf in range(2):
-                    junk = tailp.tile([P, 512], F32, name="junk", tag="junk")
-                    nc.scalar.activation(out=junk[:], in_=xts[(i, hf)][:], func=ACT.Square, bias=nm[:, 0:1], scale=1.0,
-                                         accum_out=sq[:, hf : hf + 1])
-                vr = small.tile([P, 1], F32, name="vr", tag="vr")
-                nc.gpsimd.tensor_scalar(out=vr[:], in0=sq[:, 0:1], scalar1=sq[:, 1:2], scalar2=1.0 / D, op0=ALU.add, op1=ALU.mult)
-                shift[i] = (nm[:, 0:1], ALU.add)
-                spread[i] = vr[:, 0:1]
-        for i in range(NT):
+        rstd = {}
+
+        def stats_vector(i):
+            st = small.tile([P, 2, 6], F32, name="st", tag="st")
+            for hf in range(2):
+                nc.vector.bn_stats(out=st[:, hf, :], in_=xts[(i, hf)][:])
+            mv = small.tile([P, 2], F32, name="mv", tag="mv")
+            nc.vector.bn_aggr(out=mv[:], in_=st[:].rearrange("p a b -> p (a b)"))
+            shift[i] = (mv[:, 0:1], ALU.subtract)
+            spread[i] = mv[:, 1:2]
+
+        def stats_scalar(i):
+            sm = small.tile([P, 2], F32, name="sm", tag="sm")
+            for hf in range(2):
+                junk = tailp.tile([P, 512], F32, name="junk", tag="junk")
+                nc.scalar.activation(out=junk[:], in_=xts[(i, hf)][:], func=ACT.Copy, accum_out=sm[:, hf : hf + 1])
+            nm = small.tile([P, 1], F32, name="nm", tag="nm")
+            nc.gpsimd.tensor_scalar(out=nm[:], in0=sm[:, 0:1], scalar1=sm[:, 1:2], scalar2=-1.0 / D, op0=ALU.add, op1=ALU.mult)
+            sq = small.tile([P, 2], F32, name="sq", tag="sq")
+            for hf in range(2):
+                junk = tailp.tile([P, 512], F32, name="junk", tag="junk")
+                nc.scalar.activation(out=junk[:], in_=xts[(i, hf)][:], func=ACT.Square, bias=nm[:, 0:1], scale=1.0,
+                                     accum_out=sq[:, hf : hf + 1])
+            vr = small.tile([P, 1], F32, name="vr", tag="vr")
+            nc.gpsimd.tensor_scalar(out=vr[:], in0=sq[:, 0:1], scalar1=sq[:, 1:2], scalar2=1.0 / D, op0=ALU.add, op1=ALU.mult)
+            shift[i] = (nm[:, 0:1], ALU.add)
+            spread[i] = vr[:, 0:1]
+
+        def deviation(i):
             sd = small.tile([P, 1], F32, name="sd", tag="sd")
             nc.scalar.activation(out=sd[:], in_=spread[i], func=ACT.Sqrt, bias=eps_t[:, 0:1], scale=1.0)
+            rstd[i] = sd
+
+        def normalize(i):
             rs = small.tile([P, 1], F32, name="rs", tag="rs")
-            nc.vector.reciprocal(out=rs[:], in_=sd[:])
-            t = tailp.tile([P, D], F32, name="t", tag="t")
-            for hf in range(2):
-                cols = slice(512 * hf, 512 * (hf + 1))
-                nc.vector.scalar_tensor_tensor(
-                    out=t[:, cols], in0=xts[(i, hf)][:], scalar=shift[i][0], in1=gamma_b[:, cols],
-                    op0=shift[i][1], op1=ALU.mult,
-                )
-            y = tailp.tile([P, D], F32, name="y", tag="y", bufs=3)
-            nc.vector.scalar_tensor_tensor(
-                out=y[:], in0=t[:], scalar=rs[:, 0:1], in1=beta_b[:], op0=ALU.mult, op1=ALU.add,
-            )
-            f8 = tailp.tile([P, D], FP8, name="f8", tag="f8", bufs=4)
-            nc.scalar.activation(out=f8[:], in_=y[:], func=ACT.Copy, scale=Y_SCALE, saturate=False)
+            nc.vector.reciprocal(out=rs[:], in_=rstd[i][:])
             b, i2 = divmod(i, 2)
             rows = slice(P * i2, P * (i2 + 1))
-            nc.sync.dma_start(out=out_0[b, rows, :], in_=y[:])
-            nc.sync.dma_start(out=out_1[b, rows, :], in_=f8[:].bitcast(U8))
+            ts = []
+            for hf in range(2):
+                t = tailp.tile([P, 512], F32, name="t", tag="t", bufs=4)
+                ts.append(t)
+                nc.vector.scalar_tensor_tensor(
+                    out=t[:], in0=xts[(i, hf)][:], scalar=shift[i][0], in1=gamma_b[:, 512 * hf : 512 * (hf + 1)],
+                    op0=shift[i][1], op1=ALU.mult,
+                )
+            for hf in range(2):
+                cols = slice(512 * hf, 512 * (hf + 1))
+                y = tailp.tile([P, 512], F32, name="y", tag="y", bufs=6)
+                nc.vector.scalar_tensor_tensor(
+                    out=y[:], in0=ts[hf][:], scalar=rs[:, 0:1], in1=beta_b[:, cols], op0=ALU.mult, op1=ALU.add,
+                )
+                f8 = tailp.tile([P, 512], FP8, name="f8", tag="f8", bufs=8)
+                nc.scalar.activation(out=f8[:], in_=y[:], func=ACT.Copy, scale=Y_SCALE, saturate=False)
+                nc.sync.dma_start(out=out_0[b, rows, cols], in_=y[:])
+                nc.sync.dma_start(out=out_1[b, rows, cols], in_=f8[:].bitcast(U8))
+
+        stats_scalar(3)
+        stats_vector(0)
+        deviation(0)
+        for i in range(NT):
+            if i + 1 < 3:
+                stats_vector(i + 1)
+            if i + 1 < NT:
+                deviation(i + 1)
+            normalize(i)

@@ -163,8 +163,7 @@ def tile_multiheadattentionunit_pa_kernel(tc, attn, Wo, bo, query_inputs, gamma,
                 elif e == "V":
                     nc.vector.tensor_copy(out=dst, in_=src)
                 else:
-                    nc.gpsimd.tensor_scalar(out=t[:], in0=w_raw[(h, g)][:, :, P * p0 : P * (p0 + n)].rearrange("p j d -> p d j"),
-                                            scalar1=1.0, scalar2=0.0, op0=ALU.mult, op1=ALU.add)
+                    nc.gpsimd.tensor_scalar(out=dst, in0=src, scalar1=1.0, scalar2=0.0, op0=ALU.mult, op1=ALU.add)
 
         def prepare_scalar(h):
             if not ok(h):

@@ -29,9 +29,7 @@ def shares(h, g):
     if h == 0:
         return "VVVVVSSS"
     if h == 1:
-        return "VVVSSSSS" if g == 0 else "SSSSSSGG"
-    if h == 2:
-        return "VVSSGGGG" if g == 0 else "SSSSSSGG"
+        return "VVSSSSSS" if g == 0 else "SSSSSSGG"
     return "SSSSGGGG" if g == 0 else "SSSSSSGG"
 
 
@@ -55,10 +53,6 @@ def chunks(n):
             out.append(w)
             n -= w
     return out
-
-
-def on_scalar(h, j):
-    return (h == 6 and j < 4) or (h == 7 and j >= 4)
 
 
 def tile_multiheadattentionunit_pa_kernel(tc, attn, Wo, bo, query_inputs, gamma, beta, out_0, out_1):
@@ -122,11 +116,8 @@ def tile_multiheadattentionunit_pa_kernel(tc, attn, Wo, bo, query_inputs, gamma,
         nc.vector.tensor_scalar(out=eps_t[:], in0=warm[:], scalar1=LN_EPS, scalar2=None, op0=ALU.mult)
 
         acc = const.tile([P, ND, TOK], F32, name="acc")
-        acc2 = const.tile([P, ND, TOK], F32, name="acc2")
         negb = const.tile([P, H * ND], F32, name="negb")
-        posb = const.tile([P, H * ND], F32, name="posb")
         bsum = const.tile([P, ND], F32, name="bsum")
-        bsv = const.tile([P, ND], F32, name="bsv")
         gamma_b = const.tile([P, D], BF16, name="gamma_b")
         beta_b = const.tile([P, D], BF16, name="beta_b")
         q_raw = const.tile([P, NT, D], BF16, name="q_raw")
@@ -232,11 +223,9 @@ def tile_multiheadattentionunit_pa_kernel(tc, attn, Wo, bo, query_inputs, gamma,
                 return
             for j in range(j0, j1):
                 col = slice(ND * h + j, ND * h + j + 1)
-                if on_scalar(h, j):
-                    nc.scalar.activation(out=acc2[:, j, :], in_=mxs[(h, j)][:], func=ACT.Relu, bias=posb[:, col], scale=1.0)
-                elif h == 0:
+                if h == 0:
                     nc.vector.tensor_scalar(out=acc[:, j, :], in0=mxs[(h, j)][:], scalar1=negb[:, col],
-                                            scalar2=bsv[:, j : j + 1], op0=ALU.max, op1=ALU.add)
+                                            scalar2=bsum[:, j : j + 1], op0=ALU.max, op1=ALU.add)
                 else:
                     nc.vector.scalar_tensor_tensor(out=acc[:, j, :], in0=mxs[(h, j)][:], scalar=negb[:, col],
                                                    in1=acc[:, j, :], op0=ALU.max, op1=ALU.add)
@@ -246,26 +235,23 @@ def tile_multiheadattentionunit_pa_kernel(tc, attn, Wo, bo, query_inputs, gamma,
             xts[(i, hf)] = xt
             nc.tensor.matmul(out=xt[:], lhsT=ident_b[:], rhs=q_raw[:, i, 512 * hf : 512 * (hf + 1)], start=True, stop=False)
 
-        def xt_add(i, hf, chain, last):
+        def xt_add(i, hf):
             xt = xts[(i, hf)]
             for jj in range(4):
                 nc.tensor.matmul(
                     out=xt[:, P * jj : P * (jj + 1)],
-                    lhsT=chain[:, 4 * hf + jj, P * i : P * (i + 1)],
+                    lhsT=acc[:, 4 * hf + jj, P * i : P * (i + 1)],
                     rhs=ident_f[:],
                     is_transpose=True,
                     start=False,
-                    stop=(last and jj == 3),
+                    stop=(jj == 3),
                 )
 
         cps = psum.tile([P, P], BF16, name="cps", tag="tp")
         nc.tensor.transpose(cps[:], cst[:], ident_b[:])
         nc.vector.tensor_scalar(out=negb[:], in0=cps[:, 0 : H * ND], scalar1=-1.0, scalar2=None, op0=ALU.mult)
-        nc.vector.tensor_copy(out=posb[:], in_=cps[:, 0 : H * ND])
         nc.vector.tensor_reduce(out=bsum[:], in_=cps[:, 0 : H * ND].rearrange("p (h j) -> p j h", h=H),
                                 axis=mybir.AxisListType.X, op=ALU.add)
-        nc.vector.tensor_tensor(out=bsv[:, 0:4], in0=bsum[:, 0:4], in1=posb[:, 6 * ND : 6 * ND + 4], op=ALU.subtract)
-        nc.vector.tensor_tensor(out=bsv[:, 4:8], in0=bsum[:, 4:8], in1=posb[:, 7 * ND + 4 : 7 * ND + 8], op=ALU.subtract)
 
         transpose_a(0)
         prepare_scalar(0)
@@ -292,9 +278,7 @@ def tile_multiheadattentionunit_pa_kernel(tc, attn, Wo, bo, query_inputs, gamma,
             if h == H - 1:
                 for i in range(2):
                     xt_open(i, 0, "tp")
-                    xt_add(i, 0, acc2, False)
                     xt_open(i, 1, "tp")
-                    xt_add(i, 1, acc, False)
             epilogue(h, 0, 3)
             matmuls(h, 4, 7)
             quantize(h + 1, 0)
@@ -306,11 +290,9 @@ def tile_multiheadattentionunit_pa_kernel(tc, attn, Wo, bo, query_inputs, gamma,
         for i in range(NT):
             if i >= 2:
                 xt_open(i, 0, "mx")
-                xt_add(i, 0, acc2, False)
                 xt_open(i, 1, "mx")
-                xt_add(i, 1, acc, False)
-            xt_add(i, 0, acc, True)
-            xt_add(i, 1, acc2, True)
+            xt_add(i, 0)
+            xt_add(i, 1)
 
         shift = {}
         spread = {}

from contextlib import ExitStack

import concourse.masks as masks
import concourse.mybir as mybir

B, H, S, DV, D = 2, 8, 256, 1024, 1024
FLOPS = 2 * B * H * S * DV * D

F32 = mybir.dt.float32
BF16 = mybir.dt.bfloat16
U32 = mybir.dt.uint32
U8 = mybir.dt.uint8
FP8X4 = mybir.dt.float8_e4m3fn_x4
FP8 = mybir.dt.float8_e4m3fn
ALU = mybir.AluOpType
ACT = mybir.ActivationFunctionType

P = 128
TOK = B * S
NT = TOK // P
ND = D // P
NG = DV // 512
LN_EPS = 1e-3
Y_SCALE = 220.0
AHEAD = 3


def shares(h, g):
    if h == 0:
        return "VVVVVSSS"
    if h == 1:
        return "VVSSSSSS" if g == 0 else "SSSSSSGG"
    return "SSSSGGGG" if g == 0 else "SSSSSSGG"


def runs(h, g):
    s = shares(h, g)
    out = []
    i = 0
    while i < 8:
        k = i
        while k < 8 and s[k] == s[i]:
            k += 1
        out.append((s[i], i, k - i))
        i = k
    return out


def chunks(n):
    out = []
    for w in (8, 4, 2, 1):
        while n >= w:
            out.append(w)
            n -= w
    return out


def tile_multiheadattentionunit_pa_kernel(tc, attn, Wo, bo, query_inputs, gamma, beta, out_0, out_1):
    nc = tc.nc
    with ExitStack() as ctx:
        const = ctx.enter_context(tc.tile_pool(name="const", bufs=1))
        wpool = ctx.enter_context(tc.tile_pool(name="wpool", bufs=2 * AHEAD))
        apool = ctx.enter_context(tc.tile_pool(name="apool", bufs=AHEAD))
        upool = ctx.enter_context(tc.tile_pool(name="upool", bufs=4))
        cpool = ctx.enter_context(tc.tile_pool(name="cpool", bufs=4))
        small = ctx.enter_context(tc.tile_pool(name="small", bufs=4))
        tailp = ctx.enter_context(tc.tile_pool(name="tailp", bufs=2))
        psum = ctx.enter_context(tc.psum_pool(name="psum", bufs=4))
        ctx.enter_context(tc.manual_schedule(engines={mybir.EngineType.DVE, mybir.EngineType.Pool}))

        a_raw = {}
        w_raw = {}
        tps = {}
        a_grp = {}
        a_code = {}
        a_scale = {}
        units = {}
        w_code = {}
        w_scale = {}
        mxs = {}
        xts = {}

        def ok(h):
            return 0 <= h < H

        def load_a(h):
            t = apool.tile([P, NT, DV], BF16, name="a_raw", tag="a_raw")
            a_raw[h] = t
            for b in range(B):
                nc.sync.dma_start(out=t[:, 2 * b : 2 * b + 2, :], in_=attn[b, h].rearrange("(i p) k -> p i k", p=P))

        def load_w(h):
            for g in range(NG):
                t = wpool.tile([P, 4, D], BF16, name="w_raw", tag="w_raw")
                w_raw[(h, g)] = t
                nc.sync.dma_start(out=t[:], in_=Wo[h, 512 * g : 512 * (g + 1), :].rearrange("(p j) d -> p j d", j=4))

        load_a(0)
        cst = const.tile([P, P], BF16, name="cst")
        nc.vector.memset(cst[:], 0.0)
        nc.sync.dma_start(out=cst[0:64, :], in_=bo.rearrange("h (j p) -> (h j) p", p=P))
        load_w(0)
        for h in range(1, AHEAD):
            load_a(h)
            load_w(h)

        ident_f = const.tile([P, P], F32, name="ident_f")
        masks.make_identity(nc, ident_f[:])
        ident_b = const.tile([P, P], BF16, name="ident_b")
        masks.make_identity(nc, ident_b[:])
        warm = const.tile([P, 1], F32, name="warm")
        nc.vector.memset(warm[:], 1.0)
        warm2 = const.tile([P, 1], F32, name="warm2")
        nc.scalar.activation(out=warm2[:], in_=warm[:], func=ACT.Sqrt)
        eps_t = const.tile([P, 1], F32, name="eps_t")
        nc.vector.tensor_scalar(out=eps_t[:], in0=warm[:], scalar1=LN_EPS, scalar2=None, op0=ALU.mult)

        acc = const.tile([P, ND, TOK], F32, name="acc")
        negb = const.tile([P, H * ND], F32, name="negb")
        bsum = const.tile([P, ND], F32, name="bsum")
        gamma_b = const.tile([P, D], BF16, name="gamma_b")
        beta_b = const.tile([P, D], BF16, name="beta_b")
        q_raw = const.tile([P, NT, D], BF16, name="q_raw")

        def transpose_a(h):
            if not ok(h):
                return
            words = a_raw[h][:].bitcast(F32)
            for b in range(B):
                for g in range(NG):
                    tp = psum.tile([P, 2, 256], F32, name="tp", tag="tp")
                    tps[(h, g, b)] = tp
                    for ii in range(2):
                        for u in range(2):
                            nc.tensor.transpose(
                                tp[:, u, P * ii : P * (ii + 1)],
                                words[:, 2 * b + ii, 256 * g + u : 256 * (g + 1) : 2],
                                ident_f[:],
                            )

        def interleave(h, g, e):
            if not ok(h):
                return
            for eng, p0, n in runs(h, g):
                if eng != e:
                    continue
                t = upool.tile([P, P * n, 4], BF16, name="unit" + e, tag="unit" + e,
                               bufs={"S": 4, "V": 2, "G": 1}[e], align_bytes=64)
                units[(h, g, p0)] = t
                src = w_raw[(h, g)][:, :, P * p0 : P * (p0 + n)].rearrange("p j (c i) -> p c j i", i=4)
                dst = t[:].rearrange("p (c i) j -> p c j i", i=4)
                if e == "S":
                    nc.scalar.copy(out=dst, in_=src)
                elif e == "V":
                    nc.vector.tensor_copy(out=dst, in_=src)
                else:
                    nc.gpsimd.tensor_scalar(out=dst, in0=src, scalar1=1.0, scalar2=0.0, op0=ALU.mult, op1=ALU.add)

        def prepare_scalar(h):
            if not ok(h):
                return
            w32 = {}
            for g in range(NG):
                t = cpool.tile([P, 4 * TOK], BF16, name="a_grp", tag="a_grp", align_bytes=64)
                a_grp[(h, g)] = t
                w32[g] = t[:].bitcast(F32).rearrange("p (r u) -> p r u", u=2)
            for b in range(B):
                for g in range(NG):
                    nc.scalar.copy(
                        out=w32[g][:, 256 * b : 256 * (b + 1), :],
                        in_=tps[(h, g, b)][:].rearrange("p u r -> p r u"),
                    )
            for g in range(NG):
                interleave(h, g, "S")

        def quantize(h, g):
            if not ok(h):
                return
            interleave(h, g, "V")
            c = cpool.tile([P, TOK], U32, name="a_code", tag="a_code", align_bytes=64)
            s = cpool.tile([P, TOK], U8, name="a_scale", tag="a_scale", align_bytes=64)
            a_code[(h, g)] = c
            a_scale[(h, g)] = s
            nc.vector.quantize_mx(out=c[:].bitcast(FP8X4), scales=s[:], in_=a_grp[(h, g)][:])
            wc = cpool.tile([P, D], U32, name="w_code", tag="w_code", align_bytes=64)
            ws = cpool.tile([P, D], U8, name="w_scale", tag="w_scale", align_bytes=64)
            w_code[(h, g)] = wc
            w_scale[(h, g)] = ws
            for e in ("S", "V", "G"):
                for eng, p0, n in runs(h, g):
                    if eng != e:
                        continue
                    o = 0
                    for w in chunks(n):
                        cols = slice(P * (p0 + o), P * (p0 + o + w))
                        nc.vector.quantize_mx(
                            out=wc[:, cols].bitcast(FP8X4),
                            scales=ws[:, cols],
                            in_=units[(h, g, p0)][:, P * o : P * (o + w), :].rearrange("p d j -> p (d j)"),
                        )
                        o += w

        def matmuls(h, j0, j1):
            if not ok(h):
                return
            for j in range(j0, j1):
                ps = psum.tile([P, TOK], F32, name="mx", tag="mx")
                mxs[(h, j)] = ps
                cols = slice(P * j, P * (j + 1))
                for g in range(NG):
                    nc.tensor.matmul_mx(
                        out=ps[:],
                        lhsT=w_code[(h, g)][:, cols].bitcast(FP8X4),
                        lhsT_scale=w_scale[(h, g)][:, cols],
                        rhs=a_code[(h, g)][:].bitcast(FP8X4),
                        rhs_scale=a_scale[(h, g)][:],
                        start=(g == 0),
                        stop=(g == NG - 1),
                    )

        def epilogue(h, j0, j1):
            if not ok(h):
                return
            for j in range(j0, j1):
                col = slice(ND * h + j, ND * h + j + 1)
                if h == 0:
                    nc.vector.tensor_scalar(out=acc[:, j, :], in0=mxs[(h, j)][:], scalar1=negb[:, col],
                                            scalar2=bsum[:, j : j + 1], op0=ALU.max, op1=ALU.add)
                else:
                    nc.vector.scalar_tensor_tensor(out=acc[:, j, :], in0=mxs[(h, j)][:], scalar=negb[:, col],
                                                   in1=acc[:, j, :], op0=ALU.max, op1=ALU.add)

        def xt_open(i, hf, tag):
            xt = psum.tile([P, 512], F32, name="xt", tag=tag)
            xts[(i, hf)] = xt
            nc.tensor.matmul(out=xt[:], lhsT=ident_b[:], rhs=q_raw[:, i, 512 * hf : 512 * (hf + 1)], start=True, stop=False)

        def xt_add(i, hf):
            xt = xts[(i, hf)]
            for jj in range(4):
                nc.tensor.matmul(
                    out=xt[:, P * jj : P * (jj + 1)],
                    lhsT=acc[:, 4 * hf + jj, P * i : P * (i + 1)],
                    rhs=ident_f[:],
                    is_transpose=True,
                    start=False,
                    stop=(jj == 3),
                )

        cps = psum.tile([P, P], BF16, name="cps", tag="tp")
        nc.tensor.transpose(cps[:], cst[:], ident_b[:])
        nc.vector.tensor_scalar(out=negb[:], in0=cps[:, 0 : H * ND], scalar1=-1.0, scalar2=None, op0=ALU.mult)
        nc.vector.tensor_reduce(out=bsum[:], in_=cps[:, 0 : H * ND].rearrange("p (h j) -> p j h", h=H),
                                axis=mybir.AxisListType.X, op=ALU.add)

        transpose_a(0)
        prepare_scalar(0)
        transpose_a(1)
        interleave(0, 0, "G")
        quantize(0, 0)
        interleave(0, 1, "G")
        for h in range(H):
            hl = h + AHEAD
            if ok(hl):
                load_a(hl)
                load_w(hl)
            if hl == H:
                nc.sync.dma_start(out=gamma_b[:], in_=gamma.partition_broadcast(P))
                nc.sync.dma_start(out=beta_b[:], in_=beta.partition_broadcast(P))
                for b in range(B):
                    nc.sync.dma_start(out=q_raw[:, 2 * b : 2 * b + 2, :], in_=query_inputs[b].rearrange("(i p) d -> p i d", p=P))
            prepare_scalar(h + 1)
            quantize(h, 1)
            interleave(h + 1, 0, "G")
            epilogue(h - 1, 6, 8)
            matmuls(h, 0, 4)
            transpose_a(h + 2)
            if h == H - 1:
                for i in range(2):
                    xt_open(i, 0, "tp")
                    xt_open(i, 1, "tp")
            epilogue(h, 0, 3)
            matmuls(h, 4, 7)
            quantize(h + 1, 0)
            interleave(h + 1, 1, "G")
            epilogue(h, 3, 6)
            matmuls(h, 7, 8)
        epilogue(H - 1, 6, 8)

        for i in range(NT):
            if i >= 2:
                xt_open(i, 0, "mx")
                xt_open(i, 1, "mx")
            xt_add(i, 0)
            xt_add(i, 1)

        shift = {}
        spread = {}
        rstd = {}

        def stats_vector(i):
            st = small.tile([P, 2, 6], F32, name="st", tag="st")
            for hf in range(2):
                nc.vector.bn_stats(out=st[:, hf, :], in_=xts[(i, hf)][:])
            mv = small.tile([P, 2], F32, name="mv", tag="mv")
            nc.vector.bn_aggr(out=mv[:], in_=st[:].rearrange("p a b -> p (a b)"))
            shift[i] = (mv[:, 0:1], ALU.subtract)
            spread[i] = mv[:, 1:2]

        def stats_scalar(i):
            sm = small.tile([P, 2], F32, name="sm", tag="sm")
            for hf in range(2):
                junk = tailp.tile([P, 512], F32, name="junk", tag="junk")
                nc.scalar.activation(out=junk[:], in_=xts[(i, hf)][:], func=ACT.Copy, accum_out=sm[:, hf : hf + 1])
            nm = small.tile([P, 1], F32, name="nm", tag="nm")
            nc.gpsimd.tensor_scalar(out=nm[:], in0=sm[:, 0:1], scalar1=sm[:, 1:2], scalar2=-1.0 / D, op0=ALU.add, op1=ALU.mult)
            sq = small.tile([P, 2], F32, name="sq", tag="sq")
            for hf in range(2):
                junk = tailp.tile([P, 512], F32, name="junk", tag="junk")
                nc.scalar.activation(out=junk[:], in_=xts[(i, hf)][:], func=ACT.Square, bias=nm[:, 0:1], scale=1.0,
                                     accum_out=sq[:, hf : hf + 1])
            vr = small.tile([P, 1], F32, name="vr", tag="vr")
            nc.gpsimd.tensor_scalar(out=vr[:], in0=sq[:, 0:1], scalar1=sq[:, 1:2], scalar2=1.0 / D, op0=ALU.add, op1=ALU.mult)
            shift[i] = (nm[:, 0:1], ALU.add)
            spread[i] = vr[:, 0:1]

        def deviation(i):
            sd = small.tile([P, 1], F32, name="sd", tag="sd")
            nc.scalar.activation(out=sd[:], in_=spread[i], func=ACT.Sqrt, bias=eps_t[:, 0:1], scale=1.0)
            rstd[i] = sd

        def normalize(i):
            rs = small.tile([P, 1], F32, name="rs", tag="rs")
            nc.vector.reciprocal(out=rs[:], in_=rstd[i][:])
            b, i2 = divmod(i, 2)
            rows = slice(P * i2, P * (i2 + 1))
            ts = []
            for hf in range(2):
                t = tailp.tile([P, 512], F32, name="t", tag="t", bufs=4)
                ts.append(t)
                nc.vector.scalar_tensor_tensor(
                    out=t[:], in0=xts[(i, hf)][:], scalar=shift[i][0], in1=gamma_b[:, 512 * hf : 512 * (hf + 1)],
                    op0=shift[i][1], op1=ALU.mult,
                )
            for hf in range(2):
                cols = slice(512 * hf, 512 * (hf + 1))
                y = tailp.tile([P, 512], F32, name="y", tag="y", bufs=6)
                nc.vector.scalar_tensor_tensor(
                    out=y[:], in0=ts[hf][:], scalar=rs[:, 0:1], in1=beta_b[:, cols], op0=ALU.mult, op1=ALU.add,
                )
                f8 = tailp.tile([P, 512], FP8, name="f8", tag="f8", bufs=8)
                nc.scalar.activation(out=f8[:], in_=y[:], func=ACT.Copy, scale=Y_SCALE, saturate=False)
                nc.sync.dma_start(out=out_0[b, rows, cols], in_=y[:])
                nc.sync.dma_start(out=out_1[b, rows, cols], in_=f8[:].bitcast(U8))

        stats_scalar(3)
        stats_vector(0)
        deviation(0)
        for i in range(NT):
            if i + 1 < 3:
                stats_vector(i + 1)
            if i + 1 < NT:
                deviation(i + 1)
            normalize(i)
